import numpy as np
import ml_dtypes


def mxq(x, axis, fmt="e4m3"):
    dtype, down = {"e4m3": (ml_dtypes.float8_e4m3fn, 7), "e5m2": (ml_dtypes.float8_e5m2, 14)}[fmt]
    v = np.moveaxis(np.asarray(x, np.float32).astype(ml_dtypes.bfloat16).astype(np.float64), axis, -1)
    blocks = v.reshape(v.shape[:-1] + (-1, 32))
    amax = np.abs(blocks).max(-1, keepdims=True)
    byte = np.maximum(np.where(amax > 0, np.frexp(amax)[1] - 1 + 127, 0) - down, 1)
    scale = np.exp2(byte - 127.0)
    codes = (blocks / scale).astype(np.float32).astype(dtype).astype(np.float64)
    return np.moveaxis((codes * scale).reshape(v.shape), -1, axis)


WIDE = False


def mx_kscale(k):
    if not WIDE:
        return np.ones(k)
    levels = np.array([10, -10, 5, -5, 0])
    a = np.random.permutation(np.resize(levels, k // 512 * 4)).reshape(k // 512, 4)
    idx = np.arange(k)
    return np.exp2(a[idx // 512, idx % 128 // 32])


BF16 = ml_dtypes.bfloat16


def bf(x):
    return np.asarray(x, np.float32).astype(BF16)


def f64(x):
    return np.asarray(x).astype(np.float64)


B, D, G, S, K, E, H, C1, C2, C3 = 192, 1024, 16, 128, 128, 2, 512, 8, 64, 128
EPS = 1e-5


def sigmoid(v):
    return 1.0 / (1.0 + np.exp(-v))


def setup_inputs():
    t = mx_kscale(H)
    return {"le": bf(np.maximum(np.random.standard_normal((B, G, S)), 0.0) * 1.25),
            "ew1": bf(np.random.standard_normal((E, H, S)) * 1.2 / np.sqrt(S)),
            "ew2": bf(np.random.standard_normal((E, K, H)) * 3.0 / np.sqrt(H) / t),
            "ebg": bf((1.0 + 0.1 * np.random.standard_normal((E, G, H))) * t),
            "ebb": bf(0.3 * np.random.standard_normal((E, G, H)) * t),
            "ebm": bf(0.3 * np.random.standard_normal((E, G, H))),
            "ebv": bf(0.5 + np.random.uniform(size=(E, G, H)))}


def reference(le, ew1, ew2, ebg, ebb, ebm, ebv):
    u = (f64(le).reshape(B * G, S) @ f64(ew1).transpose(0, 2, 1)).reshape(E, B, G, H)
    gain = f64(ebg) / np.sqrt(f64(ebv) + EPS)
    h = np.maximum((u - f64(ebm)[:, None]) * gain[:, None] + f64(ebb)[:, None], 0.0)
    hq = mxq(h.reshape(E, B * G, H), 2, "e4m3")
    out = (hq @ mxq(f64(ew2), 2, "e4m3").transpose(0, 2, 1)).reshape(E, B, G, K)
    sel = sigmoid(out[0])
    sel = np.clip(1.2 * sel - 0.1, 0.0, 1.0)
    layer_bias = out[E - 1]
    return sel, layer_bias

@@ -1,0 +1,263 @@
+from contextlib import ExitStack
+
+import concourse.mybir as mybir
+from concourse.masks import make_identity
+
+BF16 = mybir.dt.bfloat16
+F32 = mybir.dt.float32
+U32 = mybir.dt.uint32
+U8 = mybir.dt.uint8
+FP8X4 = mybir.dt.float8_e4m3fn_x4
+ACT = mybir.ActivationFunctionType
+ALU = mybir.AluOpType
+
+P = 128
+PACK = 4
+BATCH = 192
+GATES = 16
+FEATURES = 128
+EXPERTS = 2
+HIDDEN = 512
+OUTPUTS = 128
+EPS = 1e-5
+
+PAIRS = GATES // 2
+REST = BATCH - P
+ROW_TILES = 3
+COLS = ROW_TILES * P
+UNITS = PAIRS * EXPERTS
+BN_ROWS = EXPERTS * GATES
+
+FLOPS = 2 * 2 * EXPERTS * BATCH * GATES * FEATURES * HIDDEN
+
+
+def tile_tgnetworkbias_pa_kernel(tc, le, ew1, ew2, ebg, ebb, ebm, ebv, out_0, out_1):
+    nc = tc.nc
+    with ExitStack() as stack:
+        const = stack.enter_context(tc.tile_pool(name="const", bufs=1))
+        work = stack.enter_context(tc.tile_pool(name="work", bufs=3))
+        results = stack.enter_context(tc.tile_pool(name="results", bufs=4))
+        psum_tr = stack.enter_context(tc.psum_pool(name="psum_tr", bufs=2))
+        psum_u = stack.enter_context(tc.psum_pool(name="psum_u", bufs=4))
+        psum_o = stack.enter_context(tc.psum_pool(name="psum_o", bufs=2))
+
+        bn_rows = const.tile([P, HIDDEN], BF16)
+        for q, param in enumerate((ebv, ebg, ebm, ebb)):
+            nc.scalar.dma_start(
+                out=bn_rows[BN_ROWS * q : BN_ROWS * (q + 1), :], in_=param.rearrange("e g h -> (e g) h")
+            )
+        w1_rows = const.tile([P, EXPERTS, PACK, FEATURES], BF16)
+        nc.sync.dma_start(out=w1_rows[:], in_=ew1.rearrange("e (p t) s -> p e t s", t=PACK))
+        le_gates = le.rearrange("b (half j) s -> b half j s", half=2)
+        le_main = const.tile([P, 2, PAIRS, FEATURES], BF16)
+        le_rest = const.tile([P, PAIRS, FEATURES], BF16)
+        for js in (slice(0, PAIRS // 2), slice(PAIRS // 2, PAIRS)):
+            nc.sync.dma_start(out=le_main[:, :, js, :], in_=le_gates[0:P, :, js, :])
+            for half in range(2):
+                nc.sync.dma_start(
+                    out=le_rest[REST * half : REST * (half + 1), js, :], in_=le_gates[P:BATCH, half, js, :]
+                )
+        w2_rows = const.tile([P, EXPERTS, HIDDEN], BF16)
+        nc.sync.dma_start(out=w2_rows[:], in_=ew2.rearrange("e k h -> k e h"))
+
+        ident = const.tile([P, P], BF16)
+        make_identity(nc, ident[:])
+        eps = const.tile([P, 1], F32)
+        nc.vector.memset(eps[:], EPS)
+
+        bn_ps = psum_o.tile([P, PACK, P], BF16, tag="o")
+        bn_chunks = bn_rows[:].rearrange("r (p t) -> r t p", t=PACK)
+        for t in range(PACK):
+            nc.tensor.transpose(out=bn_ps[:, t, :], in_=bn_chunks[:, t, :], identity=ident[:])
+        std = const.tile([P, PACK, BN_ROWS], F32)
+        rstd = const.tile([P, PACK, BN_ROWS], F32)
+        gain = const.tile([P, PACK, BN_ROWS], F32)
+        mean_gain = const.tile([P, PACK, BN_ROWS], F32)
+        shift = const.tile([P, PACK, BN_ROWS], F32)
+
+        def batchnorm_constants(e):
+            mine = slice(GATES * e, GATES * (e + 1))
+            var_ps, gamma_ps, mean_ps, beta_ps = [
+                bn_ps[:, :, BN_ROWS * q + GATES * e : BN_ROWS * q + GATES * (e + 1)] for q in range(4)
+            ]
+            nc.scalar.activation(out=std[:, :, mine], in_=var_ps, func=ACT.Sqrt, bias=eps[:, 0:1], scale=1.0)
+            nc.vector.reciprocal(out=rstd[:, :, mine], in_=std[:, :, mine])
+            nc.vector.tensor_tensor(out=gain[:, :, mine], in0=gamma_ps, in1=rstd[:, :, mine], op=ALU.mult)
+            nc.vector.tensor_tensor(out=mean_gain[:, :, mine], in0=mean_ps, in1=gain[:, :, mine], op=ALU.mult)
+            nc.vector.tensor_tensor(out=shift[:, :, mine], in0=beta_ps, in1=mean_gain[:, :, mine], op=ALU.subtract)
+
+        w1T = const.tile([P, EXPERTS, PACK, P], BF16)
+        leT = const.tile([P, PAIRS, ROW_TILES, P], BF16)
+
+        def transpose_w1(e):
+            w1_ps = psum_tr.tile([P, PACK, P], BF16, tag="tr")
+            for t in range(PACK):
+                nc.tensor.transpose(out=w1_ps[:, t, :], in_=w1_rows[:, e, t, :], identity=ident[:])
+            nc.scalar.copy(out=w1T[:, e], in_=w1_ps[:])
+
+        def transpose_le(j):
+            le_ps = psum_tr.tile([P, ROW_TILES, P], BF16, tag="tr")
+            nc.tensor.transpose(out=le_ps[:, 0, :], in_=le_main[:, 0, j, :], identity=ident[:])
+            nc.tensor.transpose(out=le_ps[:, 1, :], in_=le_rest[:, j, :], identity=ident[:])
+            nc.tensor.transpose(out=le_ps[:, 2, :], in_=le_main[:, 1, j, :], identity=ident[:])
+            nc.vector.tensor_copy(out=leT[:, j], in_=le_ps[:])
+
+        in_flight = {}
+
+        def first_matmul(unit):
+            j, e = divmod(unit, EXPERTS)
+            for t in range(PACK):
+                u_ps = psum_u.tile([P, COLS], F32, tag="u")
+                nc.tensor.matmul(
+                    out=u_ps[:],
+                    lhsT=w1T[:, e, t, :],
+                    rhs=leT[:, j].rearrange("s r c -> s (r c)"),
+                    start=True,
+                    stop=True,
+                )
+                in_flight[("u", unit, t)] = u_ps
+
+        def batchnorm(unit):
+            j, e = divmod(unit, EXPERTS)
+            planes = work.tile([P, PACK, COLS], BF16, tag="planes")
+            for t in range(PACK):
+                u_ps = in_flight[("u", unit, t)]
+                for half in range(2):
+                    cols = slice(BATCH * half, BATCH * (half + 1))
+                    row = GATES * e + PAIRS * half + j
+                    if e == 1 and t == PACK - 1:
+                        nc.vector.tensor_scalar(
+                            out=planes[:, t, cols],
+                            in0=u_ps[:, cols],
+                            scalar1=gain[:, t, row : row + 1],
+                            scalar2=shift[:, t, row : row + 1],
+                            op0=ALU.mult,
+                            op1=ALU.add,
+                        )
+                    else:
+                        nc.scalar.activation(
+                            out=planes[:, t, cols],
+                            in_=u_ps[:, cols],
+                            func=ACT.Identity,
+                            scale=gain[:, t, row : row + 1],
+                            bias=shift[:, t, row : row + 1],
+                        )
+            in_flight[("planes", unit)] = planes
+
+        def regroup(unit):
+            planes = in_flight[("planes", unit)]
+            grouped = work.tile([P, COLS, PACK], BF16, tag="grouped", align_bytes=64)
+            nc.vector.tensor_scalar_max(
+                out=grouped[:].rearrange("p (c i) t -> p c t i", i=4),
+                in0=planes[:].rearrange("p t (c i) -> p c t i", i=4),
+                scalar1=0.0,
+            )
+            in_flight[("grouped", unit)] = grouped
+
+        def quantise(unit):
+            grouped = in_flight[("grouped", unit)]
+            codes = work.tile([P, COLS], U32, tag="codes", align_bytes=64)
+            scales = work.tile([P, COLS], U8, tag="scales", align_bytes=64)
+            for r in range(ROW_TILES):
+                rows = slice(P * r, P * (r + 1))
+                nc.vector.quantize_mx(
+                    out=codes[:, rows].bitcast(FP8X4),
+                    scales=scales[:, rows],
+                    in_=grouped[:, rows, :].rearrange("p c t -> p (c t)"),
+                )
+            in_flight[("codes", unit)] = (codes, scales)
+
+        def second_matmul(unit):
+            e = unit % EXPERTS
+            codes, scales = in_flight[("codes", unit)]
+            o_ps = psum_o.tile([P, ROW_TILES, OUTPUTS], F32, tag="o")
+            outs = slice(OUTPUTS * e, OUTPUTS * (e + 1))
+            for r in range(ROW_TILES):
+                rows = slice(P * r, P * (r + 1))
+                nc.tensor.matmul_mx(
+                    out=o_ps[:, r, :],
+                    lhsT=codes[:, rows].bitcast(FP8X4),
+                    lhsT_scale=scales[:, rows],
+                    rhs=w2_codes[:, outs].bitcast(FP8X4),
+                    rhs_scale=w2_scales[:, outs],
+                    start=True,
+                    stop=True,
+                )
+            in_flight[("o", unit)] = o_ps
+
+        def sigmoid(unit):
+            o_ps = in_flight[("o", unit)]
+            res = results.tile([P, ROW_TILES, OUTPUTS], F32, tag="res")
+            nc.scalar.activation(out=res[:], in_=o_ps[:], func=ACT.Sigmoid)
+            in_flight[("res", unit)] = res
+
+        def stretch_or_copy(unit):
+            if unit % EXPERTS == 0:
+                res = in_flight[("res", unit)]
+                nc.vector.tensor_scalar(
+                    out=res[:], in0=res[:], scalar1=1.2, scalar2=-0.1, op0=ALU.mult, op1=ALU.add
+                )
+            else:
+                o_ps = in_flight[("o", unit)]
+                res = results.tile([P, ROW_TILES, OUTPUTS], F32, tag="res")
+                nc.vector.tensor_copy(out=res[:], in_=o_ps[:])
+                in_flight[("res", unit)] = res
+
+        def clip_and_store(unit):
+            j, e = divmod(unit, EXPERTS)
+            res = in_flight[("res", unit)]
+            if e == 0:
+                nc.vector.tensor_scalar(
+                    out=res[:], in0=res[:], scalar1=0.0, scalar2=1.0, op0=ALU.max, op1=ALU.min
+                )
+            out_gates = (out_0, out_1)[e].rearrange("b (half j) k -> b half j k", half=2)
+            nc.sync.dma_start(out=out_gates[0:P, :, j, :], in_=res[:, 0:ROW_TILES:2, :])
+            for half in range(2):
+                nc.sync.dma_start(
+                    out=out_gates[P:BATCH, half, j, :], in_=res[REST * half : REST * (half + 1), 1, :]
+                )
+
+        batchnorm_constants(0)
+        transpose_w1(0)
+        transpose_le(0)
+        first_matmul(0)
+        batchnorm_constants(1)
+        transpose_w1(1)
+
+        w2_grouped = const.tile([P, EXPERTS, OUTPUTS, PACK], BF16, align_bytes=64)
+        w2_codes = const.tile([P, EXPERTS * OUTPUTS], U32, align_bytes=64)
+        w2_scales = const.tile([P, EXPERTS * OUTPUTS], U8, align_bytes=64)
+        for e in range(EXPERTS):
+            w2_ps = psum_tr.tile([P, PACK, OUTPUTS], BF16, tag="tr")
+            w2_chunks = w2_rows[:, e, :].rearrange("k (p t) -> k t p", t=PACK)
+            for t in range(PACK):
+                nc.tensor.transpose(out=w2_ps[:, t, :], in_=w2_chunks[:, t, :], identity=ident[:])
+            nc.vector.tensor_copy(out=w2_grouped[:, e], in_=w2_ps[:].rearrange("p t k -> p k t"))
+        nc.vector.quantize_mx(
+            out=w2_codes[:].bitcast(FP8X4),
+            scales=w2_scales[:],
+            in_=w2_grouped[:].rearrange("p e k t -> p (e k t)"),
+        )
+
+        warm = const.tile([P, 1], F32)
+        nc.scalar.activation(out=warm[:], in_=eps[:], func=ACT.Sigmoid)
+
+        for step in range(UNITS + 3):
+            if step % EXPERTS == 0 and step + 2 < UNITS:
+                transpose_le((step + 2) // EXPERTS)
+            if 0 <= step - 2 < UNITS:
+                second_matmul(step - 2)
+            if step + 1 < UNITS:
+                first_matmul(step + 1)
+            if 0 <= step - 3 and (step - 3) % EXPERTS == 0:
+                sigmoid(step - 3)
+            if 0 <= step - 1 < UNITS:
+                regroup(step - 1)
+            if step < UNITS:
+                batchnorm(step)
+            if 0 <= step - 3:
+                stretch_or_copy(step - 3)
+            if 0 <= step - 1 < UNITS:
+                quantise(step - 1)
+            if 0 <= step - 3:
+                clip_and_store(step - 3)

@@ -34,6 +34,7 @@ FLOPS = 2 * 2 * EXPERTS * BATCH * GATES * FEATURES * HIDDEN
 def tile_tgnetworkbias_pa_kernel(tc, le, ew1, ew2, ebg, ebb, ebm, ebv, out_0, out_1):
     nc = tc.nc
     with ExitStack() as stack:
+        stack.enter_context(tc.manual_schedule())
         const = stack.enter_context(tc.tile_pool(name="const", bufs=1))
         work = stack.enter_context(tc.tile_pool(name="work", bufs=3))
         results = stack.enter_context(tc.tile_pool(name="results", bufs=4))
@@ -67,8 +68,6 @@ def tile_tgnetworkbias_pa_kernel(tc, le, ew1, ew2, ebg, ebb, ebm, ebv, out_0, ou
 
         bn_ps = psum_o.tile([P, PACK, P], BF16, tag="o")
         bn_chunks = bn_rows[:].rearrange("r (p t) -> r t p", t=PACK)
-        for t in range(PACK):
-            nc.tensor.transpose(out=bn_ps[:, t, :], in_=bn_chunks[:, t, :], identity=ident[:])
         std = const.tile([P, PACK, BN_ROWS], F32)
         rstd = const.tile([P, PACK, BN_ROWS], F32)
         gain = const.tile([P, PACK, BN_ROWS], F32)
@@ -86,6 +85,8 @@ def tile_tgnetworkbias_pa_kernel(tc, le, ew1, ew2, ebg, ebb, ebm, ebv, out_0, ou
             nc.vector.tensor_tensor(out=mean_gain[:, :, mine], in0=mean_ps, in1=gain[:, :, mine], op=ALU.mult)
             nc.vector.tensor_tensor(out=shift[:, :, mine], in0=beta_ps, in1=mean_gain[:, :, mine], op=ALU.subtract)
 
+        in_flight = {}
+
         w1T = const.tile([P, EXPERTS, PACK, P], BF16)
         leT = const.tile([P, PAIRS, ROW_TILES, P], BF16)
 
@@ -93,16 +94,17 @@ def tile_tgnetworkbias_pa_kernel(tc, le, ew1, ew2, ebg, ebb, ebm, ebv, out_0, ou
             w1_ps = psum_tr.tile([P, PACK, P], BF16, tag="tr")
             for t in range(PACK):
                 nc.tensor.transpose(out=w1_ps[:, t, :], in_=w1_rows[:, e, t, :], identity=ident[:])
-            nc.scalar.copy(out=w1T[:, e], in_=w1_ps[:])
+            nc.vector.tensor_copy(out=w1T[:, e], in_=w1_ps[:])
 
         def transpose_le(j):
             le_ps = psum_tr.tile([P, ROW_TILES, P], BF16, tag="tr")
             nc.tensor.transpose(out=le_ps[:, 0, :], in_=le_main[:, 0, j, :], identity=ident[:])
             nc.tensor.transpose(out=le_ps[:, 1, :], in_=le_rest[:, j, :], identity=ident[:])
             nc.tensor.transpose(out=le_ps[:, 2, :], in_=le_main[:, 1, j, :], identity=ident[:])
-            nc.vector.tensor_copy(out=leT[:, j], in_=le_ps[:])
+            in_flight[("le", j)] = le_ps
 
-        in_flight = {}
+        def copy_le(j):
+            nc.vector.tensor_copy(out=leT[:, j], in_=in_flight[("le", j)][:])
 
         def first_matmul(unit):
             j, e = divmod(unit, EXPERTS)
@@ -217,22 +219,25 @@ def tile_tgnetworkbias_pa_kernel(tc, le, ew1, ew2, ebg, ebb, ebm, ebv, out_0, ou
                     out=out_gates[P:BATCH, half, j, :], in_=res[REST * half : REST * (half + 1), 1, :]
                 )
 
-        batchnorm_constants(0)
         transpose_w1(0)
         transpose_le(0)
+        copy_le(0)
+        for t in range(PACK):
+            nc.tensor.transpose(out=bn_ps[:, t, :], in_=bn_chunks[:, t, :], identity=ident[:])
         first_matmul(0)
-        batchnorm_constants(1)
+        batchnorm_constants(0)
         transpose_w1(1)
+        batchnorm_constants(1)
 
         w2_grouped = const.tile([P, EXPERTS, OUTPUTS, PACK], BF16, align_bytes=64)
         w2_codes = const.tile([P, EXPERTS * OUTPUTS], U32, align_bytes=64)
         w2_scales = const.tile([P, EXPERTS * OUTPUTS], U8, align_bytes=64)
+        w2_ps = psum_tr.tile([P, EXPERTS, PACK, OUTPUTS], BF16, tag="tr")
+        w2_chunks = w2_rows[:].rearrange("k e (p t) -> k e t p", t=PACK)
         for e in range(EXPERTS):
-            w2_ps = psum_tr.tile([P, PACK, OUTPUTS], BF16, tag="tr")
-            w2_chunks = w2_rows[:, e, :].rearrange("k (p t) -> k t p", t=PACK)
             for t in range(PACK):
-                nc.tensor.transpose(out=w2_ps[:, t, :], in_=w2_chunks[:, t, :], identity=ident[:])
-            nc.vector.tensor_copy(out=w2_grouped[:, e], in_=w2_ps[:].rearrange("p t k -> p k t"))
+                nc.tensor.transpose(out=w2_ps[:, e, t, :], in_=w2_chunks[:, e, t, :], identity=ident[:])
+        nc.vector.tensor_copy(out=w2_grouped[:], in_=w2_ps[:].rearrange("p e t k -> p e k t"))
         nc.vector.quantize_mx(
             out=w2_codes[:].bitcast(FP8X4),
             scales=w2_scales[:],
@@ -261,3 +266,5 @@ def tile_tgnetworkbias_pa_kernel(tc, le, ew1, ew2, ebg, ebb, ebm, ebv, out_0, ou
                 quantise(step - 1)
             if 0 <= step - 3:
                 clip_and_store(step - 3)
+            if step % EXPERTS == 0 and step + 2 < UNITS:
+                copy_le((step + 2) // EXPERTS)

@@ -187,23 +187,18 @@ def tile_tgnetworkbias_pa_kernel(tc, le, ew1, ew2, ebg, ebb, ebm, ebv, out_0, ou
                 )
             in_flight[("o", unit)] = o_ps
 
-        def sigmoid(unit):
+        def leave_psum(unit):
             o_ps = in_flight[("o", unit)]
             res = results.tile([P, ROW_TILES, OUTPUTS], F32, tag="res")
-            nc.scalar.activation(out=res[:], in_=o_ps[:], func=ACT.Sigmoid)
+            if unit % EXPERTS == 0:
+                nc.scalar.activation(out=res[:], in_=o_ps[:], func=ACT.Sigmoid)
+            else:
+                nc.scalar.copy(out=res[:], in_=o_ps[:])
             in_flight[("res", unit)] = res
 
-        def stretch_or_copy(unit):
-            if unit % EXPERTS == 0:
-                res = in_flight[("res", unit)]
-                nc.vector.tensor_scalar(
-                    out=res[:], in0=res[:], scalar1=1.2, scalar2=-0.1, op0=ALU.mult, op1=ALU.add
-                )
-            else:
-                o_ps = in_flight[("o", unit)]
-                res = results.tile([P, ROW_TILES, OUTPUTS], F32, tag="res")
-                nc.vector.tensor_copy(out=res[:], in_=o_ps[:])
-                in_flight[("res", unit)] = res
+        def stretch(unit):
+            res = in_flight[("res", unit)]
+            nc.vector.tensor_scalar(out=res[:], in0=res[:], scalar1=1.2, scalar2=-0.1, op0=ALU.mult, op1=ALU.add)
 
         def clip_and_store(unit):
             j, e = divmod(unit, EXPERTS)
@@ -254,17 +249,17 @@ def tile_tgnetworkbias_pa_kernel(tc, le, ew1, ew2, ebg, ebb, ebm, ebv, out_0, ou
                 second_matmul(step - 2)
             if step + 1 < UNITS:
                 first_matmul(step + 1)
-            if 0 <= step - 3 and (step - 3) % EXPERTS == 0:
-                sigmoid(step - 3)
+            if 0 <= step - 3:
+                leave_psum(step - 3)
             if 0 <= step - 1 < UNITS:
                 regroup(step - 1)
             if step < UNITS:
                 batchnorm(step)
-            if 0 <= step - 3:
-                stretch_or_copy(step - 3)
+            if step % EXPERTS == 0 and step + 2 < UNITS:
+                copy_le((step + 2) // EXPERTS)
+            if 0 <= step - 3 and (step - 3) % EXPERTS == 0:
+                stretch(step - 3)
             if 0 <= step - 1 < UNITS:
                 quantise(step - 1)
             if 0 <= step - 3:
                 clip_and_store(step - 3)
-            if step % EXPERTS == 0 and step + 2 < UNITS:
-                copy_le((step + 2) // EXPERTS)

@@ -44,7 +44,7 @@ def tile_tgnetworkbias_pa_kernel(tc, le, ew1, ew2, ebg, ebb, ebm, ebv, out_0, ou
 
         bn_rows = const.tile([P, HIDDEN], BF16)
         for q, param in enumerate((ebv, ebg, ebm, ebb)):
-            nc.scalar.dma_start(
+            (nc.sync, nc.scalar)[q % 2].dma_start(
                 out=bn_rows[BN_ROWS * q : BN_ROWS * (q + 1), :], in_=param.rearrange("e g h -> (e g) h")
             )
         w1_rows = const.tile([P, EXPERTS, PACK, FEATURES], BF16)
@@ -74,13 +74,19 @@ def tile_tgnetworkbias_pa_kernel(tc, le, ew1, ew2, ebg, ebb, ebm, ebv, out_0, ou
         mean_gain = const.tile([P, PACK, BN_ROWS], F32)
         shift = const.tile([P, PACK, BN_ROWS], F32)
 
-        def batchnorm_constants(e):
+        def bn_parameter(q, e):
+            return bn_ps[:, :, BN_ROWS * q + GATES * e : BN_ROWS * q + GATES * (e + 1)]
+
+        def reciprocal_std(e):
             mine = slice(GATES * e, GATES * (e + 1))
-            var_ps, gamma_ps, mean_ps, beta_ps = [
-                bn_ps[:, :, BN_ROWS * q + GATES * e : BN_ROWS * q + GATES * (e + 1)] for q in range(4)
-            ]
-            nc.scalar.activation(out=std[:, :, mine], in_=var_ps, func=ACT.Sqrt, bias=eps[:, 0:1], scale=1.0)
+            nc.scalar.activation(
+                out=std[:, :, mine], in_=bn_parameter(0, e), func=ACT.Sqrt, bias=eps[:, 0:1], scale=1.0
+            )
             nc.vector.reciprocal(out=rstd[:, :, mine], in_=std[:, :, mine])
+
+        def gain_and_shift(e):
+            mine = slice(GATES * e, GATES * (e + 1))
+            gamma_ps, mean_ps, beta_ps = bn_parameter(1, e), bn_parameter(2, e), bn_parameter(3, e)
             nc.vector.tensor_tensor(out=gain[:, :, mine], in0=gamma_ps, in1=rstd[:, :, mine], op=ALU.mult)
             nc.vector.tensor_tensor(out=mean_gain[:, :, mine], in0=mean_ps, in1=gain[:, :, mine], op=ALU.mult)
             nc.vector.tensor_tensor(out=shift[:, :, mine], in0=beta_ps, in1=mean_gain[:, :, mine], op=ALU.subtract)
@@ -160,8 +166,7 @@ def tile_tgnetworkbias_pa_kernel(tc, le, ew1, ew2, ebg, ebb, ebm, ebv, out_0, ou
             grouped = in_flight[("grouped", unit)]
             codes = work.tile([P, COLS], U32, tag="codes", align_bytes=64)
             scales = work.tile([P, COLS], U8, tag="scales", align_bytes=64)
-            for r in range(ROW_TILES):
-                rows = slice(P * r, P * (r + 1))
+            for rows in (slice(0, 2 * P), slice(2 * P, 3 * P)):
                 nc.vector.quantize_mx(
                     out=codes[:, rows].bitcast(FP8X4),
                     scales=scales[:, rows],
@@ -214,15 +219,17 @@ def tile_tgnetworkbias_pa_kernel(tc, le, ew1, ew2, ebg, ebb, ebm, ebv, out_0, ou
                     out=out_gates[P:BATCH, half, j, :], in_=res[REST * half : REST * (half + 1), 1, :]
                 )
 
+        for t in range(PACK):
+            nc.tensor.transpose(out=bn_ps[:, t, :], in_=bn_chunks[:, t, :], identity=ident[:])
+        reciprocal_std(0)
         transpose_w1(0)
         transpose_le(0)
         copy_le(0)
-        for t in range(PACK):
-            nc.tensor.transpose(out=bn_ps[:, t, :], in_=bn_chunks[:, t, :], identity=ident[:])
         first_matmul(0)
-        batchnorm_constants(0)
+        gain_and_shift(0)
+        reciprocal_std(1)
         transpose_w1(1)
-        batchnorm_constants(1)
+        gain_and_shift(1)
 
         w2_grouped = const.tile([P, EXPERTS, OUTPUTS, PACK], BF16, align_bytes=64)
         w2_codes = const.tile([P, EXPERTS * OUTPUTS], U32, align_bytes=64)

@@ -110,7 +110,7 @@ def tile_tgnetworkbias_pa_kernel(tc, le, ew1, ew2, ebg, ebb, ebm, ebv, out_0, ou
             in_flight[("le", j)] = le_ps
 
         def copy_le(j):
-            nc.vector.tensor_copy(out=leT[:, j], in_=in_flight[("le", j)][:])
+            nc.scalar.copy(out=leT[:, j], in_=in_flight[("le", j)][:])
 
         def first_matmul(unit):
             j, e = divmod(unit, EXPERTS)
@@ -133,7 +133,7 @@ def tile_tgnetworkbias_pa_kernel(tc, le, ew1, ew2, ebg, ebb, ebm, ebv, out_0, ou
                 for half in range(2):
                     cols = slice(BATCH * half, BATCH * (half + 1))
                     row = GATES * e + PAIRS * half + j
-                    if e == 1 and t == PACK - 1:
+                    if t == PACK - 1:
                         nc.vector.tensor_scalar(
                             out=planes[:, t, cols],
                             in0=u_ps[:, cols],
@@ -203,14 +203,14 @@ def tile_tgnetworkbias_pa_kernel(tc, le, ew1, ew2, ebg, ebb, ebm, ebv, out_0, ou
 
         def stretch(unit):
             res = in_flight[("res", unit)]
-            nc.vector.tensor_scalar(out=res[:], in0=res[:], scalar1=1.2, scalar2=-0.1, op0=ALU.mult, op1=ALU.add)
+            nc.gpsimd.tensor_scalar(out=res[:], in0=res[:], scalar1=1.2, scalar2=-0.1, op0=ALU.mult, op1=ALU.add)
 
         def clip_and_store(unit):
             j, e = divmod(unit, EXPERTS)
             res = in_flight[("res", unit)]
             if e == 0:
-                nc.vector.tensor_scalar(
-                    out=res[:], in0=res[:], scalar1=0.0, scalar2=1.0, op0=ALU.max, op1=ALU.min
+                nc.gpsimd.tensor_scalar(
+                    out=res[:], in0=res[:], scalar1=1.0, scalar2=0.0, op0=ALU.min, op1=ALU.max
                 )
             out_gates = (out_0, out_1)[e].rearrange("b (half j) k -> b half j k", half=2)
             nc.sync.dma_start(out=out_gates[0:P, :, j, :], in_=res[:, 0:ROW_TILES:2, :])
@@ -224,7 +224,7 @@ def tile_tgnetworkbias_pa_kernel(tc, le, ew1, ew2, ebg, ebb, ebm, ebv, out_0, ou
         reciprocal_std(0)
         transpose_w1(0)
         transpose_le(0)
-        copy_le(0)
+        nc.vector.tensor_copy(out=leT[:, 0], in_=in_flight[("le", 0)][:])
         first_matmul(0)
         gain_and_shift(0)
         reciprocal_std(1)

@@ -27,6 +27,8 @@ ROW_TILES = 3
 COLS = ROW_TILES * P
 UNITS = PAIRS * EXPERTS
 BN_ROWS = EXPERTS * GATES
+WARM_COLS = 512
+WARM_PASSES = 4
 
 FLOPS = 2 * 2 * EXPERTS * BATCH * GATES * FEATURES * HIDDEN
 
@@ -48,23 +50,39 @@ def tile_tgnetworkbias_pa_kernel(tc, le, ew1, ew2, ebg, ebb, ebm, ebv, out_0, ou
                 out=bn_rows[BN_ROWS * q : BN_ROWS * (q + 1), :], in_=param.rearrange("e g h -> (e g) h")
             )
         w1_rows = const.tile([P, EXPERTS, PACK, FEATURES], BF16)
-        nc.sync.dma_start(out=w1_rows[:], in_=ew1.rearrange("e (p t) s -> p e t s", t=PACK))
+        w1_units = ew1.rearrange("e (p t) s -> p e t s", t=PACK)
         le_gates = le.rearrange("b (half j) s -> b half j s", half=2)
         le_main = const.tile([P, 2, PAIRS, FEATURES], BF16)
         le_rest = const.tile([P, PAIRS, FEATURES], BF16)
-        for js in (slice(0, PAIRS // 2), slice(PAIRS // 2, PAIRS)):
-            nc.sync.dma_start(out=le_main[:, :, js, :], in_=le_gates[0:P, :, js, :])
-            for half in range(2):
-                nc.sync.dma_start(
-                    out=le_rest[REST * half : REST * (half + 1), js, :], in_=le_gates[P:BATCH, half, js, :]
-                )
+        le_rest_rows = le[P:BATCH].rearrange("r (half j) s -> (r half) j s", half=2)
         w2_rows = const.tile([P, EXPERTS, HIDDEN], BF16)
+
+        def load_le(js):
+            nc.sync.dma_start(out=le_main[:, :, js, :], in_=le_gates[0:P, :, js, :])
+            nc.sync.dma_start(out=le_rest[:, js, :], in_=le_rest_rows[:, js, :])
+
+        nc.sync.dma_start(out=w1_rows[:, 0], in_=w1_units[:, 0])
+        load_le(slice(0, 1))
+        nc.sync.dma_start(out=w1_rows[:, 1], in_=w1_units[:, 1])
         nc.sync.dma_start(out=w2_rows[:], in_=ew2.rearrange("e k h -> k e h"))
+        load_le(slice(1, 2))
+        load_le(slice(2, PAIRS))
+
+        zeros = const.tile([P, WARM_COLS], BF16)
+        nc.vector.memset(zeros[:], 0.0)
+        eps = const.tile([P, 1], F32)
+        nc.vector.memset(eps[:], EPS)
+        warm_ps = psum_u.tile([P, WARM_COLS], F32, tag="u")
+        for warm_pass in range(WARM_PASSES):
+            nc.tensor.matmul(out=warm_ps[:], lhsT=zeros[:, 0:P], rhs=zeros[:], start=True, stop=True)
 
         ident = const.tile([P, P], BF16)
         make_identity(nc, ident[:])
-        eps = const.tile([P, 1], F32)
-        nc.vector.memset(eps[:], EPS)
+        unzip = const.tile([P, P], BF16)
+        nc.gpsimd.tensor_copy(
+            out=unzip[:].rearrange("k (half r) -> k half r", half=2),
+            in_=ident[:].rearrange("k (r half) -> k half r", half=2),
+        )
 
         bn_ps = psum_o.tile([P, PACK, P], BF16, tag="o")
         bn_chunks = bn_rows[:].rearrange("r (p t) -> r t p", t=PACK)
@@ -74,22 +92,8 @@ def tile_tgnetworkbias_pa_kernel(tc, le, ew1, ew2, ebg, ebb, ebm, ebv, out_0, ou
         mean_gain = const.tile([P, PACK, BN_ROWS], F32)
         shift = const.tile([P, PACK, BN_ROWS], F32)
 
-        def bn_parameter(q, e):
-            return bn_ps[:, :, BN_ROWS * q + GATES * e : BN_ROWS * q + GATES * (e + 1)]
-
-        def reciprocal_std(e):
-            mine = slice(GATES * e, GATES * (e + 1))
-            nc.scalar.activation(
-                out=std[:, :, mine], in_=bn_parameter(0, e), func=ACT.Sqrt, bias=eps[:, 0:1], scale=1.0
-            )
-            nc.vector.reciprocal(out=rstd[:, :, mine], in_=std[:, :, mine])
-
-        def gain_and_shift(e):
-            mine = slice(GATES * e, GATES * (e + 1))
-            gamma_ps, mean_ps, beta_ps = bn_parameter(1, e), bn_parameter(2, e), bn_parameter(3, e)
-            nc.vector.tensor_tensor(out=gain[:, :, mine], in0=gamma_ps, in1=rstd[:, :, mine], op=ALU.mult)
-            nc.vector.tensor_tensor(out=mean_gain[:, :, mine], in0=mean_ps, in1=gain[:, :, mine], op=ALU.mult)
-            nc.vector.tensor_tensor(out=shift[:, :, mine], in0=beta_ps, in1=mean_gain[:, :, mine], op=ALU.subtract)
+        def bn_parameter(q):
+            return bn_ps[:, :, BN_ROWS * q : BN_ROWS * (q + 1)]
 
         in_flight = {}
 
@@ -100,12 +104,15 @@ def tile_tgnetworkbias_pa_kernel(tc, le, ew1, ew2, ebg, ebb, ebm, ebv, out_0, ou
             w1_ps = psum_tr.tile([P, PACK, P], BF16, tag="tr")
             for t in range(PACK):
                 nc.tensor.transpose(out=w1_ps[:, t, :], in_=w1_rows[:, e, t, :], identity=ident[:])
-            nc.vector.tensor_copy(out=w1T[:, e], in_=w1_ps[:])
+            in_flight[("w1", e)] = w1_ps
+
+        def copy_w1(e):
+            nc.vector.tensor_copy(out=w1T[:, e], in_=in_flight[("w1", e)][:])
 
         def transpose_le(j):
             le_ps = psum_tr.tile([P, ROW_TILES, P], BF16, tag="tr")
             nc.tensor.transpose(out=le_ps[:, 0, :], in_=le_main[:, 0, j, :], identity=ident[:])
-            nc.tensor.transpose(out=le_ps[:, 1, :], in_=le_rest[:, j, :], identity=ident[:])
+            nc.tensor.transpose(out=le_ps[:, 1, :], in_=le_rest[:, j, :], identity=unzip[:])
             nc.tensor.transpose(out=le_ps[:, 2, :], in_=le_main[:, 1, j, :], identity=ident[:])
             in_flight[("le", j)] = le_ps
 
@@ -127,13 +134,14 @@ def tile_tgnetworkbias_pa_kernel(tc, le, ew1, ew2, ebg, ebb, ebm, ebv, out_0, ou
 
         def batchnorm(unit):
             j, e = divmod(unit, EXPERTS)
+            vector_takes = 2 if unit == 0 else 1
             planes = work.tile([P, PACK, COLS], BF16, tag="planes")
             for t in range(PACK):
                 u_ps = in_flight[("u", unit, t)]
                 for half in range(2):
                     cols = slice(BATCH * half, BATCH * (half + 1))
                     row = GATES * e + PAIRS * half + j
-                    if t == PACK - 1:
+                    if t >= PACK - vector_takes:
                         nc.vector.tensor_scalar(
                             out=planes[:, t, cols],
                             in0=u_ps[:, cols],
@@ -221,36 +229,50 @@ def tile_tgnetworkbias_pa_kernel(tc, le, ew1, ew2, ebg, ebb, ebm, ebv, out_0, ou
 
         for t in range(PACK):
             nc.tensor.transpose(out=bn_ps[:, t, :], in_=bn_chunks[:, t, :], identity=ident[:])
-        reciprocal_std(0)
+        nc.scalar.activation(out=std[:], in_=bn_parameter(0), func=ACT.Sqrt, bias=eps[:, 0:1], scale=1.0)
+        warm = const.tile([P, 1], F32)
+        nc.scalar.activation(out=warm[:], in_=eps[:], func=ACT.Sigmoid)
         transpose_w1(0)
         transpose_le(0)
+        copy_w1(0)
+        nc.vector.reciprocal(out=rstd[:], in_=std[:])
         nc.vector.tensor_copy(out=leT[:, 0], in_=in_flight[("le", 0)][:])
-        first_matmul(0)
-        gain_and_shift(0)
-        reciprocal_std(1)
         transpose_w1(1)
-        gain_and_shift(1)
+        transpose_le(1)
+        first_matmul(0)
+        nc.vector.tensor_tensor(out=gain[:], in0=bn_parameter(1), in1=rstd[:], op=ALU.mult)
+        nc.vector.tensor_tensor(out=mean_gain[:], in0=bn_parameter(2), in1=gain[:], op=ALU.mult)
+        copy_w1(1)
+        nc.vector.tensor_tensor(out=shift[:], in0=bn_parameter(3), in1=mean_gain[:], op=ALU.subtract)
+        nc.vector.tensor_copy(out=leT[:, 1], in_=in_flight[("le", 1)][:])
 
         w2_grouped = const.tile([P, EXPERTS, OUTPUTS, PACK], BF16, align_bytes=64)
         w2_codes = const.tile([P, EXPERTS * OUTPUTS], U32, align_bytes=64)
         w2_scales = const.tile([P, EXPERTS * OUTPUTS], U8, align_bytes=64)
-        w2_ps = psum_tr.tile([P, EXPERTS, PACK, OUTPUTS], BF16, tag="tr")
         w2_chunks = w2_rows[:].rearrange("k e (p t) -> k e t p", t=PACK)
-        for e in range(EXPERTS):
-            for t in range(PACK):
-                nc.tensor.transpose(out=w2_ps[:, e, t, :], in_=w2_chunks[:, e, t, :], identity=ident[:])
-        nc.vector.tensor_copy(out=w2_grouped[:], in_=w2_ps[:].rearrange("p e t k -> p e k t"))
-        nc.vector.quantize_mx(
-            out=w2_codes[:].bitcast(FP8X4),
-            scales=w2_scales[:],
-            in_=w2_grouped[:].rearrange("p e k t -> p (e k t)"),
-        )
 
-        warm = const.tile([P, 1], F32)
-        nc.scalar.activation(out=warm[:], in_=eps[:], func=ACT.Sigmoid)
+        def transpose_w2():
+            w2_ps = psum_o.tile([P, EXPERTS, PACK, OUTPUTS], BF16, tag="o")
+            for e in range(EXPERTS):
+                for t in range(PACK):
+                    nc.tensor.transpose(out=w2_ps[:, e, t, :], in_=w2_chunks[:, e, t, :], identity=ident[:])
+            in_flight["w2"] = w2_ps
+
+        def regroup_w2():
+            nc.vector.tensor_copy(out=w2_grouped[:], in_=in_flight["w2"][:].rearrange("p e t k -> p e k t"))
+
+        def quantise_w2():
+            nc.vector.quantize_mx(
+                out=w2_codes[:].bitcast(FP8X4),
+                scales=w2_scales[:],
+                in_=w2_grouped[:].rearrange("p e k t -> p (e k t)"),
+            )
+
+        transpose_w2()
 
         for step in range(UNITS + 3):
-            if step % EXPERTS == 0 and step + 2 < UNITS:
+            turn_le = step % EXPERTS == 0 and 2 <= step and step + 2 < UNITS
+            if turn_le:
                 transpose_le((step + 2) // EXPERTS)
             if 0 <= step - 2 < UNITS:
                 second_matmul(step - 2)
@@ -262,11 +284,15 @@ def tile_tgnetworkbias_pa_kernel(tc, le, ew1, ew2, ebg, ebb, ebm, ebv, out_0, ou
                 regroup(step - 1)
             if step < UNITS:
                 batchnorm(step)
-            if step % EXPERTS == 0 and step + 2 < UNITS:
+            if step == 1:
+                regroup_w2()
+            if turn_le:
                 copy_le((step + 2) // EXPERTS)
             if 0 <= step - 3 and (step - 3) % EXPERTS == 0:
                 stretch(step - 3)
             if 0 <= step - 1 < UNITS:
                 quantise(step - 1)
+            if step == 1:
+                quantise_w2()
             if 0 <= step - 3:
                 clip_and_store(step - 3)

@@ -13,6 +13,7 @@ ALU = mybir.AluOpType
 
 P = 128
 PACK = 4
+WORDS = PACK // 2
 BATCH = 192
 GATES = 16
 FEATURES = 128
@@ -76,24 +77,29 @@ def tile_tgnetworkbias_pa_kernel(tc, le, ew1, ew2, ebg, ebb, ebm, ebv, out_0, ou
         for warm_pass in range(WARM_PASSES):
             nc.tensor.matmul(out=warm_ps[:], lhsT=zeros[:, 0:P], rhs=zeros[:], start=True, stop=True)
 
+        ident_words = const.tile([P, P], F32)
+        make_identity(nc, ident_words[:])
         ident = const.tile([P, P], BF16)
-        make_identity(nc, ident[:])
+        nc.vector.tensor_copy(out=ident[:], in_=ident_words[:])
         unzip = const.tile([P, P], BF16)
-        nc.gpsimd.tensor_copy(
+        nc.vector.tensor_copy(
             out=unzip[:].rearrange("k (half r) -> k half r", half=2),
-            in_=ident[:].rearrange("k (r half) -> k half r", half=2),
+            in_=ident_words[:].rearrange("k (r half) -> k half r", half=2),
         )
 
-        bn_ps = psum_o.tile([P, PACK, P], BF16, tag="o")
-        bn_chunks = bn_rows[:].rearrange("r (p t) -> r t p", t=PACK)
-        std = const.tile([P, PACK, BN_ROWS], F32)
-        rstd = const.tile([P, PACK, BN_ROWS], F32)
-        gain = const.tile([P, PACK, BN_ROWS], F32)
-        mean_gain = const.tile([P, PACK, BN_ROWS], F32)
-        shift = const.tile([P, PACK, BN_ROWS], F32)
+        bn_ps = psum_o.tile([P, WORDS, P], F32, tag="o")
+        bn_words = bn_rows[:].bitcast(F32)
+        bn_values = (
+            bn_ps[:].rearrange("p u r -> p (u r)").bitcast(BF16).rearrange("p (u r v) -> p u r v", u=WORDS, v=2)
+        )
+        std = const.tile([P, WORDS, BN_ROWS, 2], F32)
+        rstd = const.tile([P, WORDS, BN_ROWS, 2], F32)
+        gain = const.tile([P, WORDS, BN_ROWS, 2], F32)
+        mean_gain = const.tile([P, WORDS, BN_ROWS, 2], F32)
+        shift = const.tile([P, WORDS, BN_ROWS, 2], F32)
 
         def bn_parameter(q):
-            return bn_ps[:, :, BN_ROWS * q : BN_ROWS * (q + 1)]
+            return bn_values[:, :, BN_ROWS * q : BN_ROWS * (q + 1), :]
 
         in_flight = {}
 
@@ -145,8 +151,8 @@ def tile_tgnetworkbias_pa_kernel(tc, le, ew1, ew2, ebg, ebb, ebm, ebv, out_0, ou
                         nc.vector.tensor_scalar(
                             out=planes[:, t, cols],
                             in0=u_ps[:, cols],
-                            scalar1=gain[:, t, row : row + 1],
-                            scalar2=shift[:, t, row : row + 1],
+                            scalar1=gain[:, t // 2, row, t % 2 : t % 2 + 1],
+                            scalar2=shift[:, t // 2, row, t % 2 : t % 2 + 1],
                             op0=ALU.mult,
                             op1=ALU.add,
                         )
@@ -155,8 +161,8 @@ def tile_tgnetworkbias_pa_kernel(tc, le, ew1, ew2, ebg, ebb, ebm, ebv, out_0, ou
                             out=planes[:, t, cols],
                             in_=u_ps[:, cols],
                             func=ACT.Identity,
-                            scale=gain[:, t, row : row + 1],
-                            bias=shift[:, t, row : row + 1],
+                            scale=gain[:, t // 2, row, t % 2 : t % 2 + 1],
+                            bias=shift[:, t // 2, row, t % 2 : t % 2 + 1],
                         )
             in_flight[("planes", unit)] = planes
 
@@ -227,8 +233,8 @@ def tile_tgnetworkbias_pa_kernel(tc, le, ew1, ew2, ebg, ebb, ebm, ebv, out_0, ou
                     out=out_gates[P:BATCH, half, j, :], in_=res[REST * half : REST * (half + 1), 1, :]
                 )
 
-        for t in range(PACK):
-            nc.tensor.transpose(out=bn_ps[:, t, :], in_=bn_chunks[:, t, :], identity=ident[:])
+        for u in range(WORDS):
+            nc.tensor.transpose(out=bn_ps[:, u, :], in_=bn_words[:, u : HIDDEN // 2 : WORDS], identity=ident_words[:])
         nc.scalar.activation(out=std[:], in_=bn_parameter(0), func=ACT.Sqrt, bias=eps[:, 0:1], scale=1.0)
         warm = const.tile([P, 1], F32)
         nc.scalar.activation(out=warm[:], in_=eps[:], func=ACT.Sigmoid)
@@ -249,17 +255,25 @@ def tile_tgnetworkbias_pa_kernel(tc, le, ew1, ew2, ebg, ebb, ebm, ebv, out_0, ou
         w2_grouped = const.tile([P, EXPERTS, OUTPUTS, PACK], BF16, align_bytes=64)
         w2_codes = const.tile([P, EXPERTS * OUTPUTS], U32, align_bytes=64)
         w2_scales = const.tile([P, EXPERTS * OUTPUTS], U8, align_bytes=64)
-        w2_chunks = w2_rows[:].rearrange("k e (p t) -> k e t p", t=PACK)
+        w2_words = w2_rows[:].rearrange("k e h -> k (e h)").bitcast(F32).rearrange("k (e w) -> k e w", e=EXPERTS)
 
         def transpose_w2():
-            w2_ps = psum_o.tile([P, EXPERTS, PACK, OUTPUTS], BF16, tag="o")
+            w2_ps = psum_o.tile([P, EXPERTS, WORDS, OUTPUTS], F32, tag="o")
             for e in range(EXPERTS):
-                for t in range(PACK):
-                    nc.tensor.transpose(out=w2_ps[:, e, t, :], in_=w2_chunks[:, e, t, :], identity=ident[:])
+                for u in range(WORDS):
+                    nc.tensor.transpose(
+                        out=w2_ps[:, e, u, :], in_=w2_words[:, e, u : HIDDEN // 2 : WORDS], identity=ident_words[:]
+                    )
             in_flight["w2"] = w2_ps
 
         def regroup_w2():
-            nc.vector.tensor_copy(out=w2_grouped[:], in_=in_flight["w2"][:].rearrange("p e t k -> p e k t"))
+            nc.vector.tensor_copy(
+                out=w2_grouped[:]
+                .rearrange("p e k t -> p (e k t)")
+                .bitcast(F32)
+                .rearrange("p (e k u) -> p e k u", e=EXPERTS, u=WORDS),
+                in_=in_flight["w2"][:].rearrange("p e u k -> p e k u"),
+            )
 
         def quantise_w2():
             nc.vector.quantize_mx(

@@ -28,8 +28,8 @@ ROW_TILES = 3
 COLS = ROW_TILES * P
 UNITS = PAIRS * EXPERTS
 BN_ROWS = EXPERTS * GATES
-WARM_COLS = 512
-WARM_PASSES = 4
+WARM_COLS = 128
+WARM_PASSES = 13
 
 FLOPS = 2 * 2 * EXPERTS * BATCH * GATES * FEATURES * HIDDEN
 
@@ -69,13 +69,19 @@ def tile_tgnetworkbias_pa_kernel(tc, le, ew1, ew2, ebg, ebb, ebm, ebv, out_0, ou
         load_le(slice(1, 2))
         load_le(slice(2, PAIRS))
 
-        zeros = const.tile([P, WARM_COLS], BF16)
+        zeros = const.tile([P, 2], BF16)
         nc.vector.memset(zeros[:], 0.0)
         eps = const.tile([P, 1], F32)
         nc.vector.memset(eps[:], EPS)
         warm_ps = psum_u.tile([P, WARM_COLS], F32, tag="u")
         for warm_pass in range(WARM_PASSES):
-            nc.tensor.matmul(out=warm_ps[:], lhsT=zeros[:, 0:P], rhs=zeros[:], start=True, stop=True)
+            nc.tensor.matmul(
+                out=warm_ps[:],
+                lhsT=zeros[:, 0:1].to_broadcast([P, P]),
+                rhs=zeros[:, 0:1].to_broadcast([P, WARM_COLS]),
+                start=True,
+                stop=True,
+            )
 
         ident_words = const.tile([P, P], F32)
         make_identity(nc, ident_words[:])
@@ -92,7 +98,6 @@ def tile_tgnetworkbias_pa_kernel(tc, le, ew1, ew2, ebg, ebb, ebm, ebv, out_0, ou
         bn_values = (
             bn_ps[:].rearrange("p u r -> p (u r)").bitcast(BF16).rearrange("p (u r v) -> p u r v", u=WORDS, v=2)
         )
-        std = const.tile([P, WORDS, BN_ROWS, 2], F32)
         rstd = const.tile([P, WORDS, BN_ROWS, 2], F32)
         gain = const.tile([P, WORDS, BN_ROWS, 2], F32)
         mean_gain = const.tile([P, WORDS, BN_ROWS, 2], F32)
@@ -107,7 +112,7 @@ def tile_tgnetworkbias_pa_kernel(tc, le, ew1, ew2, ebg, ebb, ebm, ebv, out_0, ou
         leT = const.tile([P, PAIRS, ROW_TILES, P], BF16)
 
         def transpose_w1(e):
-            w1_ps = psum_tr.tile([P, PACK, P], BF16, tag="tr")
+            w1_ps = (psum_u, psum_tr)[e].tile([P, PACK, P], BF16, tag=("u", "tr")[e], name="w1_ps")
             for t in range(PACK):
                 nc.tensor.transpose(out=w1_ps[:, t, :], in_=w1_rows[:, e, t, :], identity=ident[:])
             in_flight[("w1", e)] = w1_ps
@@ -217,13 +222,13 @@ def tile_tgnetworkbias_pa_kernel(tc, le, ew1, ew2, ebg, ebb, ebm, ebv, out_0, ou
 
         def stretch(unit):
             res = in_flight[("res", unit)]
-            nc.gpsimd.tensor_scalar(out=res[:], in0=res[:], scalar1=1.2, scalar2=-0.1, op0=ALU.mult, op1=ALU.add)
+            (nc.vector if unit == UNITS - 2 else nc.gpsimd).tensor_scalar(out=res[:], in0=res[:], scalar1=1.2, scalar2=-0.1, op0=ALU.mult, op1=ALU.add)
 
         def clip_and_store(unit):
             j, e = divmod(unit, EXPERTS)
             res = in_flight[("res", unit)]
             if e == 0:
-                nc.gpsimd.tensor_scalar(
+                (nc.vector if unit == UNITS - 2 else nc.gpsimd).tensor_scalar(
                     out=res[:], in0=res[:], scalar1=1.0, scalar2=0.0, op0=ALU.min, op1=ALU.max
                 )
             out_gates = (out_0, out_1)[e].rearrange("b (half j) k -> b half j k", half=2)
@@ -235,22 +240,25 @@ def tile_tgnetworkbias_pa_kernel(tc, le, ew1, ew2, ebg, ebb, ebm, ebv, out_0, ou
 
         for u in range(WORDS):
             nc.tensor.transpose(out=bn_ps[:, u, :], in_=bn_words[:, u : HIDDEN // 2 : WORDS], identity=ident_words[:])
-        nc.scalar.activation(out=std[:], in_=bn_parameter(0), func=ACT.Sqrt, bias=eps[:, 0:1], scale=1.0)
+        nc.scalar.activation(
+            out=rstd[:], in_=bn_parameter(0), func=ACT.Abs_reciprocal_sqrt, bias=eps[:, 0:1], scale=1.0
+        )
         warm = const.tile([P, 1], F32)
         nc.scalar.activation(out=warm[:], in_=eps[:], func=ACT.Sigmoid)
         transpose_w1(0)
         transpose_le(0)
         copy_w1(0)
-        nc.vector.reciprocal(out=rstd[:], in_=std[:])
-        nc.vector.tensor_copy(out=leT[:, 0], in_=in_flight[("le", 0)][:])
         transpose_w1(1)
-        transpose_le(1)
-        first_matmul(0)
         nc.vector.tensor_tensor(out=gain[:], in0=bn_parameter(1), in1=rstd[:], op=ALU.mult)
+        nc.vector.tensor_copy(out=leT[:, 0], in_=in_flight[("le", 0)][:])
+        first_matmul(0)
         nc.vector.tensor_tensor(out=mean_gain[:], in0=bn_parameter(2), in1=gain[:], op=ALU.mult)
-        copy_w1(1)
+        nc.vector.tensor_copy(out=w1T[:, 1], in_=in_flight[("w1", 1)][:])
+        transpose_le(1)
         nc.vector.tensor_tensor(out=shift[:], in0=bn_parameter(3), in1=mean_gain[:], op=ALU.subtract)
-        nc.vector.tensor_copy(out=leT[:, 1], in_=in_flight[("le", 1)][:])
+
+        def copy_le1():
+            nc.vector.tensor_copy(out=leT[:, 1], in_=in_flight[("le", 1)][:])
 
         w2_grouped = const.tile([P, EXPERTS, OUTPUTS, PACK], BF16, align_bytes=64)
         w2_codes = const.tile([P, EXPERTS * OUTPUTS], U32, align_bytes=64)
@@ -267,7 +275,7 @@ def tile_tgnetworkbias_pa_kernel(tc, le, ew1, ew2, ebg, ebb, ebm, ebv, out_0, ou
             in_flight["w2"] = w2_ps
 
         def regroup_w2():
-            nc.vector.tensor_copy(
+            nc.scalar.copy(
                 out=w2_grouped[:]
                 .rearrange("p e k t -> p (e k t)")
                 .bitcast(F32)
@@ -298,8 +306,9 @@ def tile_tgnetworkbias_pa_kernel(tc, le, ew1, ew2, ebg, ebb, ebm, ebv, out_0, ou
                 regroup(step - 1)
             if step < UNITS:
                 batchnorm(step)
-            if step == 1:
+            if step == 0:
                 regroup_w2()
+                copy_le1()
             if turn_le:
                 copy_le((step + 2) // EXPERTS)
             if 0 <= step - 3 and (step - 3) % EXPERTS == 0:

@@ -111,14 +111,14 @@ def tile_tgnetworkbias_pa_kernel(tc, le, ew1, ew2, ebg, ebb, ebm, ebv, out_0, ou
         w1T = const.tile([P, EXPERTS, PACK, P], BF16)
         leT = const.tile([P, PAIRS, ROW_TILES, P], BF16)
 
-        def transpose_w1(e):
-            w1_ps = (psum_u, psum_tr)[e].tile([P, PACK, P], BF16, tag=("u", "tr")[e], name="w1_ps")
-            for t in range(PACK):
-                nc.tensor.transpose(out=w1_ps[:, t, :], in_=w1_rows[:, e, t, :], identity=ident[:])
-            in_flight[("w1", e)] = w1_ps
+        def transpose_w1(e, ts):
+            w1_ps = (psum_u, psum_tr)[e].tile([P, len(ts), P], BF16, tag=("u", "tr")[e], name="w1_ps")
+            for place, t in enumerate(ts):
+                nc.tensor.transpose(out=w1_ps[:, place, :], in_=w1_rows[:, e, t, :], identity=ident[:])
+            in_flight[("w1", e, ts)] = w1_ps
 
-        def copy_w1(e):
-            nc.vector.tensor_copy(out=w1T[:, e], in_=in_flight[("w1", e)][:])
+        def copy_w1(e, ts):
+            nc.vector.tensor_copy(out=w1T[:, e, ts[0] : ts[-1] + 1], in_=in_flight[("w1", e, ts)][:])
 
         def transpose_le(j):
             le_ps = psum_tr.tile([P, ROW_TILES, P], BF16, tag="tr")
@@ -145,14 +145,14 @@ def tile_tgnetworkbias_pa_kernel(tc, le, ew1, ew2, ebg, ebb, ebm, ebv, out_0, ou
 
         def batchnorm(unit):
             j, e = divmod(unit, EXPERTS)
-            vector_takes = 2 if unit == 0 else 1
+            vector_ts = (1, 3) if unit == 0 else (3,)
             planes = work.tile([P, PACK, COLS], BF16, tag="planes")
             for t in range(PACK):
                 u_ps = in_flight[("u", unit, t)]
                 for half in range(2):
                     cols = slice(BATCH * half, BATCH * (half + 1))
                     row = GATES * e + PAIRS * half + j
-                    if t >= PACK - vector_takes:
+                    if t in vector_ts:
                         nc.vector.tensor_scalar(
                             out=planes[:, t, cols],
                             in0=u_ps[:, cols],
@@ -245,17 +245,20 @@ def tile_tgnetworkbias_pa_kernel(tc, le, ew1, ew2, ebg, ebb, ebm, ebv, out_0, ou
         )
         warm = const.tile([P, 1], F32)
         nc.scalar.activation(out=warm[:], in_=eps[:], func=ACT.Sigmoid)
-        transpose_w1(0)
+        early, late, both = (0, 1), (2, 3), (0, 1, 2, 3)
+        transpose_w1(0, early)
         transpose_le(0)
-        copy_w1(0)
-        transpose_w1(1)
+        transpose_w1(0, late)
         nc.vector.tensor_tensor(out=gain[:], in0=bn_parameter(1), in1=rstd[:], op=ALU.mult)
+        copy_w1(0, early)
+        transpose_w1(1, both)
         nc.vector.tensor_copy(out=leT[:, 0], in_=in_flight[("le", 0)][:])
-        first_matmul(0)
         nc.vector.tensor_tensor(out=mean_gain[:], in0=bn_parameter(2), in1=gain[:], op=ALU.mult)
-        nc.vector.tensor_copy(out=w1T[:, 1], in_=in_flight[("w1", 1)][:])
+        copy_w1(0, late)
+        first_matmul(0)
         transpose_le(1)
         nc.vector.tensor_tensor(out=shift[:], in0=bn_parameter(3), in1=mean_gain[:], op=ALU.subtract)
+        copy_w1(1, both)
 
         def copy_le1():
             nc.vector.tensor_copy(out=leT[:, 1], in_=in_flight[("le", 1)][:])
@@ -290,7 +293,6 @@ def tile_tgnetworkbias_pa_kernel(tc, le, ew1, ew2, ebg, ebb, ebm, ebv, out_0, ou
                 in_=w2_grouped[:].rearrange("p e k t -> p (e k t)"),
             )
 
-        transpose_w2()
 
         for step in range(UNITS + 3):
             turn_le = step % EXPERTS == 0 and 2 <= step and step + 2 < UNITS
@@ -300,6 +302,8 @@ def tile_tgnetworkbias_pa_kernel(tc, le, ew1, ew2, ebg, ebb, ebm, ebv, out_0, ou
                 second_matmul(step - 2)
             if step + 1 < UNITS:
                 first_matmul(step + 1)
+            if step == 0:
+                transpose_w2()
             if 0 <= step - 3:
                 leave_psum(step - 3)
             if 0 <= step - 1 < UNITS:
@@ -307,8 +311,9 @@ def tile_tgnetworkbias_pa_kernel(tc, le, ew1, ew2, ebg, ebb, ebm, ebv, out_0, ou
             if step < UNITS:
                 batchnorm(step)
             if step == 0:
-                regroup_w2()
                 copy_le1()
+            if step == 1:
+                regroup_w2()
             if turn_le:
                 copy_le((step + 2) // EXPERTS)
             if 0 <= step - 3 and (step - 3) % EXPERTS == 0:

@@ -40,7 +40,7 @@ def tile_tgnetworkbias_pa_kernel(tc, le, ew1, ew2, ebg, ebb, ebm, ebv, out_0, ou
         stack.enter_context(tc.manual_schedule())
         const = stack.enter_context(tc.tile_pool(name="const", bufs=1))
         work = stack.enter_context(tc.tile_pool(name="work", bufs=3))
-        results = stack.enter_context(tc.tile_pool(name="results", bufs=4))
+        results = stack.enter_context(tc.tile_pool(name="results", bufs=8))
         psum_tr = stack.enter_context(tc.psum_pool(name="psum_tr", bufs=2))
         psum_u = stack.enter_context(tc.psum_pool(name="psum_u", bufs=4))
         psum_o = stack.enter_context(tc.psum_pool(name="psum_o", bufs=2))
@@ -181,6 +181,18 @@ def tile_tgnetworkbias_pa_kernel(tc, le, ew1, ew2, ebg, ebb, ebm, ebv, out_0, ou
             )
             in_flight[("grouped", unit)] = grouped
 
+        def regroup_shared(unit):
+            planes = in_flight[("planes", unit)]
+            grouped = work.tile([P, COLS, PACK], BF16, tag="grouped", align_bytes=64)
+            for cols in (slice(0, 2 * P), slice(2 * P, 3 * P)):
+                out = grouped[:, cols, :].rearrange("p (c i) t -> p c t i", i=4)
+                columns = planes[:, :, cols].rearrange("p t (c i) -> p c t i", i=4)
+                if cols.start == 0:
+                    nc.vector.tensor_scalar_max(out=out, in0=columns, scalar1=0.0)
+                else:
+                    nc.scalar.activation(out=out, in_=columns, func=ACT.Relu)
+            in_flight[("grouped", unit)] = grouped
+
         def quantise(unit):
             grouped = in_flight[("grouped", unit)]
             codes = work.tile([P, COLS], U32, tag="codes", align_bytes=64)
@@ -249,8 +261,8 @@ def tile_tgnetworkbias_pa_kernel(tc, le, ew1, ew2, ebg, ebb, ebm, ebv, out_0, ou
         transpose_w1(0, early)
         transpose_le(0)
         transpose_w1(0, late)
-        nc.vector.tensor_tensor(out=gain[:], in0=bn_parameter(1), in1=rstd[:], op=ALU.mult)
         copy_w1(0, early)
+        nc.vector.tensor_tensor(out=gain[:], in0=bn_parameter(1), in1=rstd[:], op=ALU.mult)
         transpose_w1(1, both)
         nc.vector.tensor_copy(out=leT[:, 0], in_=in_flight[("le", 0)][:])
         nc.vector.tensor_tensor(out=mean_gain[:], in0=bn_parameter(2), in1=gain[:], op=ALU.mult)
@@ -278,7 +290,7 @@ def tile_tgnetworkbias_pa_kernel(tc, le, ew1, ew2, ebg, ebb, ebm, ebv, out_0, ou
             in_flight["w2"] = w2_ps
 
         def regroup_w2():
-            nc.scalar.copy(
+            nc.vector.tensor_copy(
                 out=w2_grouped[:]
                 .rearrange("p e k t -> p (e k t)")
                 .bitcast(F32)
@@ -306,8 +318,10 @@ def tile_tgnetworkbias_pa_kernel(tc, le, ew1, ew2, ebg, ebb, ebm, ebv, out_0, ou
                 transpose_w2()
             if 0 <= step - 3:
                 leave_psum(step - 3)
-            if 0 <= step - 1 < UNITS:
+            if 0 <= step - 1 < UNITS - 1:
                 regroup(step - 1)
+            if step == UNITS:
+                regroup_shared(step - 1)
             if step < UNITS:
                 batchnorm(step)
             if step == 0:

@@ -246,9 +246,15 @@ def tile_tgnetworkbias_pa_kernel(tc, le, ew1, ew2, ebg, ebb, ebm, ebv, out_0, ou
             out_gates = (out_0, out_1)[e].rearrange("b (half j) k -> b half j k", half=2)
             nc.sync.dma_start(out=out_gates[0:P, :, j, :], in_=res[:, 0:ROW_TILES:2, :])
             for half in range(2):
-                nc.sync.dma_start(
-                    out=out_gates[P:BATCH, half, j, :], in_=res[REST * half : REST * (half + 1), 1, :]
-                )
+                if half == 0 or unit < UNITS - 2:
+                    nc.sync.dma_start(
+                        out=out_gates[P:BATCH, half, j, :], in_=res[REST * half : REST * (half + 1), 1, :]
+                    )
+
+        def store_on_scalar(unit):
+            j, e = divmod(unit, EXPERTS)
+            out_gates = (out_0, out_1)[e].rearrange("b (half j) k -> b half j k", half=2)
+            nc.scalar.dma_start(out=out_gates[P:BATCH, 1, j, :], in_=in_flight[("res", unit)][REST : 2 * REST, 1, :])
 
         for u in range(WORDS):
             nc.tensor.transpose(out=bn_ps[:, u, :], in_=bn_words[:, u : HIDDEN // 2 : WORDS], identity=ident_words[:])
@@ -290,7 +296,7 @@ def tile_tgnetworkbias_pa_kernel(tc, le, ew1, ew2, ebg, ebb, ebm, ebv, out_0, ou
             in_flight["w2"] = w2_ps
 
         def regroup_w2():
-            nc.vector.tensor_copy(
+            nc.scalar.copy(
                 out=w2_grouped[:]
                 .rearrange("p e k t -> p (e k t)")
                 .bitcast(F32)
@@ -338,3 +344,5 @@ def tile_tgnetworkbias_pa_kernel(tc, le, ew1, ew2, ebg, ebb, ebm, ebv, out_0, ou
                 quantise_w2()
             if 0 <= step - 3:
                 clip_and_store(step - 3)
+        for unit in (UNITS - 2, UNITS - 1):
+            store_on_scalar(unit)

@@ -41,8 +41,8 @@ def tile_tgnetworkbias_pa_kernel(tc, le, ew1, ew2, ebg, ebb, ebm, ebv, out_0, ou
         const = stack.enter_context(tc.tile_pool(name="const", bufs=1))
         work = stack.enter_context(tc.tile_pool(name="work", bufs=3))
         results = stack.enter_context(tc.tile_pool(name="results", bufs=8))
-        psum_tr = stack.enter_context(tc.psum_pool(name="psum_tr", bufs=2))
-        psum_u = stack.enter_context(tc.psum_pool(name="psum_u", bufs=4))
+        psum_tr = stack.enter_context(tc.psum_pool(name="psum_tr", bufs=1))
+        psum_u = stack.enter_context(tc.psum_pool(name="psum_u", bufs=5))
         psum_o = stack.enter_context(tc.psum_pool(name="psum_o", bufs=2))
 
         bn_rows = const.tile([P, HIDDEN], BF16)
@@ -65,9 +65,9 @@ def tile_tgnetworkbias_pa_kernel(tc, le, ew1, ew2, ebg, ebb, ebm, ebv, out_0, ou
         nc.sync.dma_start(out=w1_rows[:, 0], in_=w1_units[:, 0])
         load_le(slice(0, 1))
         nc.sync.dma_start(out=w1_rows[:, 1], in_=w1_units[:, 1])
-        nc.sync.dma_start(out=w2_rows[:], in_=ew2.rearrange("e k h -> k e h"))
         load_le(slice(1, 2))
-        load_le(slice(2, PAIRS))
+        load_le(slice(2, 4))
+        load_le(slice(4, 8))
 
         zeros = const.tile([P, 2], BF16)
         nc.vector.memset(zeros[:], 0.0)
@@ -85,6 +85,7 @@ def tile_tgnetworkbias_pa_kernel(tc, le, ew1, ew2, ebg, ebb, ebm, ebv, out_0, ou
 
         ident_words = const.tile([P, P], F32)
         make_identity(nc, ident_words[:])
+        nc.gpsimd.dma_start(out=w2_rows[:], in_=ew2.rearrange("e k h -> k e h"))
         ident = const.tile([P, P], BF16)
         nc.vector.tensor_copy(out=ident[:], in_=ident_words[:])
         unzip = const.tile([P, P], BF16)
@@ -112,7 +113,7 @@ def tile_tgnetworkbias_pa_kernel(tc, le, ew1, ew2, ebg, ebb, ebm, ebv, out_0, ou
         leT = const.tile([P, PAIRS, ROW_TILES, P], BF16)
 
         def transpose_w1(e, ts):
-            w1_ps = (psum_u, psum_tr)[e].tile([P, len(ts), P], BF16, tag=("u", "tr")[e], name="w1_ps")
+            w1_ps = psum_u.tile([P, len(ts), P], BF16, tag="u", name="w1_ps")
             for place, t in enumerate(ts):
                 nc.tensor.transpose(out=w1_ps[:, place, :], in_=w1_rows[:, e, t, :], identity=ident[:])
             in_flight[("w1", e, ts)] = w1_ps
@@ -246,15 +247,9 @@ def tile_tgnetworkbias_pa_kernel(tc, le, ew1, ew2, ebg, ebb, ebm, ebv, out_0, ou
             out_gates = (out_0, out_1)[e].rearrange("b (half j) k -> b half j k", half=2)
             nc.sync.dma_start(out=out_gates[0:P, :, j, :], in_=res[:, 0:ROW_TILES:2, :])
             for half in range(2):
-                if half == 0 or unit < UNITS - 2:
-                    nc.sync.dma_start(
-                        out=out_gates[P:BATCH, half, j, :], in_=res[REST * half : REST * (half + 1), 1, :]
-                    )
-
-        def store_on_scalar(unit):
-            j, e = divmod(unit, EXPERTS)
-            out_gates = (out_0, out_1)[e].rearrange("b (half j) k -> b half j k", half=2)
-            nc.scalar.dma_start(out=out_gates[P:BATCH, 1, j, :], in_=in_flight[("res", unit)][REST : 2 * REST, 1, :])
+                nc.sync.dma_start(
+                    out=out_gates[P:BATCH, half, j, :], in_=res[REST * half : REST * (half + 1), 1, :]
+                )
 
         for u in range(WORDS):
             nc.tensor.transpose(out=bn_ps[:, u, :], in_=bn_words[:, u : HIDDEN // 2 : WORDS], identity=ident_words[:])
@@ -344,5 +339,3 @@ def tile_tgnetworkbias_pa_kernel(tc, le, ew1, ew2, ebg, ebb, ebm, ebv, out_0, ou
                 quantise_w2()
             if 0 <= step - 3:
                 clip_and_store(step - 3)
-        for unit in (UNITS - 2, UNITS - 1):
-            store_on_scalar(unit)

from contextlib import ExitStack

import concourse.mybir as mybir
from concourse.masks import make_identity

BF16 = mybir.dt.bfloat16
F32 = mybir.dt.float32
U32 = mybir.dt.uint32
U8 = mybir.dt.uint8
FP8X4 = mybir.dt.float8_e4m3fn_x4
ACT = mybir.ActivationFunctionType
ALU = mybir.AluOpType

P = 128
PACK = 4
WORDS = PACK // 2
BATCH = 192
GATES = 16
FEATURES = 128
EXPERTS = 2
HIDDEN = 512
OUTPUTS = 128
EPS = 1e-5

PAIRS = GATES // 2
REST = BATCH - P
ROW_TILES = 3
COLS = ROW_TILES * P
UNITS = PAIRS * EXPERTS
BN_ROWS = EXPERTS * GATES
WARM_COLS = 128
WARM_PASSES = 13

FLOPS = 2 * 2 * EXPERTS * BATCH * GATES * FEATURES * HIDDEN


def tile_tgnetworkbias_pa_kernel(tc, le, ew1, ew2, ebg, ebb, ebm, ebv, out_0, out_1):
    nc = tc.nc
    with ExitStack() as stack:
        stack.enter_context(tc.manual_schedule())
        const = stack.enter_context(tc.tile_pool(name="const", bufs=1))
        work = stack.enter_context(tc.tile_pool(name="work", bufs=3))
        results = stack.enter_context(tc.tile_pool(name="results", bufs=8))
        psum_tr = stack.enter_context(tc.psum_pool(name="psum_tr", bufs=1))
        psum_u = stack.enter_context(tc.psum_pool(name="psum_u", bufs=5))
        psum_o = stack.enter_context(tc.psum_pool(name="psum_o", bufs=2))

        bn_rows = const.tile([P, HIDDEN], BF16)
        for q, param in enumerate((ebv, ebg, ebm, ebb)):
            (nc.sync, nc.scalar)[q % 2].dma_start(
                out=bn_rows[BN_ROWS * q : BN_ROWS * (q + 1), :], in_=param.rearrange("e g h -> (e g) h")
            )
        w1_rows = const.tile([P, EXPERTS, PACK, FEATURES], BF16)
        w1_units = ew1.rearrange("e (p t) s -> p e t s", t=PACK)
        le_gates = le.rearrange("b (half j) s -> b half j s", half=2)
        le_main = const.tile([P, 2, PAIRS, FEATURES], BF16)
        le_rest = const.tile([P, PAIRS, FEATURES], BF16)
        le_rest_rows = le[P:BATCH].rearrange("r (half j) s -> (r half) j s", half=2)
        w2_rows = const.tile([P, EXPERTS, HIDDEN], BF16)

        def load_le(js):
            nc.sync.dma_start(out=le_main[:, :, js, :], in_=le_gates[0:P, :, js, :])
            nc.sync.dma_start(out=le_rest[:, js, :], in_=le_rest_rows[:, js, :])

        nc.sync.dma_start(out=w1_rows[:, 0], in_=w1_units[:, 0])
        load_le(slice(0, 1))
        nc.sync.dma_start(out=w1_rows[:, 1], in_=w1_units[:, 1])
        load_le(slice(1, 2))
        load_le(slice(2, 4))
        load_le(slice(4, 8))

        zeros = const.tile([P, 2], BF16)
        nc.vector.memset(zeros[:], 0.0)
        eps = const.tile([P, 1], F32)
        nc.vector.memset(eps[:], EPS)
        warm_ps = psum_u.tile([P, WARM_COLS], F32, tag="u")
        for warm_pass in range(WARM_PASSES):
            nc.tensor.matmul(
                out=warm_ps[:],
                lhsT=zeros[:, 0:1].to_broadcast([P, P]),
                rhs=zeros[:, 0:1].to_broadcast([P, WARM_COLS]),
                start=True,
                stop=True,
            )

        ident_words = const.tile([P, P], F32)
        make_identity(nc, ident_words[:])
        nc.gpsimd.dma_start(out=w2_rows[:], in_=ew2.rearrange("e k h -> k e h"))
        ident = const.tile([P, P], BF16)
        nc.vector.tensor_copy(out=ident[:], in_=ident_words[:])
        unzip = const.tile([P, P], BF16)
        nc.vector.tensor_copy(
            out=unzip[:].rearrange("k (half r) -> k half r", half=2),
            in_=ident_words[:].rearrange("k (r half) -> k half r", half=2),
        )

        bn_ps = psum_o.tile([P, WORDS, P], F32, tag="o")
        bn_words = bn_rows[:].bitcast(F32)
        bn_values = (
            bn_ps[:].rearrange("p u r -> p (u r)").bitcast(BF16).rearrange("p (u r v) -> p u r v", u=WORDS, v=2)
        )
        rstd = const.tile([P, WORDS, BN_ROWS, 2], F32)
        gain = const.tile([P, WORDS, BN_ROWS, 2], F32)
        mean_gain = const.tile([P, WORDS, BN_ROWS, 2], F32)
        shift = const.tile([P, WORDS, BN_ROWS, 2], F32)

        def bn_parameter(q):
            return bn_values[:, :, BN_ROWS * q : BN_ROWS * (q + 1), :]

        in_flight = {}

        w1T = const.tile([P, EXPERTS, PACK, P], BF16)
        leT = const.tile([P, PAIRS, ROW_TILES, P], BF16)

        def transpose_w1(e, ts):
            w1_ps = psum_u.tile([P, len(ts), P], BF16, tag="u", name="w1_ps")
            for place, t in enumerate(ts):
                nc.tensor.transpose(out=w1_ps[:, place, :], in_=w1_rows[:, e, t, :], identity=ident[:])
            in_flight[("w1", e, ts)] = w1_ps

        def copy_w1(e, ts):
            nc.vector.tensor_copy(out=w1T[:, e, ts[0] : ts[-1] + 1], in_=in_flight[("w1", e, ts)][:])

        def transpose_le(j):
            le_ps = psum_tr.tile([P, ROW_TILES, P], BF16, tag="tr")
            nc.tensor.transpose(out=le_ps[:, 0, :], in_=le_main[:, 0, j, :], identity=ident[:])
            nc.tensor.transpose(out=le_ps[:, 1, :], in_=le_rest[:, j, :], identity=unzip[:])
            nc.tensor.transpose(out=le_ps[:, 2, :], in_=le_main[:, 1, j, :], identity=ident[:])
            in_flight[("le", j)] = le_ps

        def copy_le(j):
            nc.scalar.copy(out=leT[:, j], in_=in_flight[("le", j)][:])

        def first_matmul(unit):
            j, e = divmod(unit, EXPERTS)
            for t in range(PACK):
                u_ps = psum_u.tile([P, COLS], F32, tag="u")
                nc.tensor.matmul(
                    out=u_ps[:],
                    lhsT=w1T[:, e, t, :],
                    rhs=leT[:, j].rearrange("s r c -> s (r c)"),
                    start=True,
                    stop=True,
                )
                in_flight[("u", unit, t)] = u_ps

        def batchnorm(unit):
            j, e = divmod(unit, EXPERTS)
            vector_ts = (1, 3) if unit == 0 else (3,)
            planes = work.tile([P, PACK, COLS], BF16, tag="planes")
            for t in range(PACK):
                u_ps = in_flight[("u", unit, t)]
                for half in range(2):
                    cols = slice(BATCH * half, BATCH * (half + 1))
                    row = GATES * e + PAIRS * half + j
                    if t in vector_ts:
                        nc.vector.tensor_scalar(
                            out=planes[:, t, cols],
                            in0=u_ps[:, cols],
                            scalar1=gain[:, t // 2, row, t % 2 : t % 2 + 1],
                            scalar2=shift[:, t // 2, row, t % 2 : t % 2 + 1],
                            op0=ALU.mult,
                            op1=ALU.add,
                        )
                    else:
                        nc.scalar.activation(
                            out=planes[:, t, cols],
                            in_=u_ps[:, cols],
                            func=ACT.Identity,
                            scale=gain[:, t // 2, row, t % 2 : t % 2 + 1],
                            bias=shift[:, t // 2, row, t % 2 : t % 2 + 1],
                        )
            in_flight[("planes", unit)] = planes

        def regroup(unit):
            planes = in_flight[("planes", unit)]
            grouped = work.tile([P, COLS, PACK], BF16, tag="grouped", align_bytes=64)
            nc.vector.tensor_scalar_max(
                out=grouped[:].rearrange("p (c i) t -> p c t i", i=4),
                in0=planes[:].rearrange("p t (c i) -> p c t i", i=4),
                scalar1=0.0,
            )
            in_flight[("grouped", unit)] = grouped

        def regroup_shared(unit):
            planes = in_flight[("planes", unit)]
            grouped = work.tile([P, COLS, PACK], BF16, tag="grouped", align_bytes=64)
            for cols in (slice(0, 2 * P), slice(2 * P, 3 * P)):
                out = grouped[:, cols, :].rearrange("p (c i) t -> p c t i", i=4)
                columns = planes[:, :, cols].rearrange("p t (c i) -> p c t i", i=4)
                if cols.start == 0:
                    nc.vector.tensor_scalar_max(out=out, in0=columns, scalar1=0.0)
                else:
                    nc.scalar.activation(out=out, in_=columns, func=ACT.Relu)
            in_flight[("grouped", unit)] = grouped

        def quantise(unit):
            grouped = in_flight[("grouped", unit)]
            codes = work.tile([P, COLS], U32, tag="codes", align_bytes=64)
            scales = work.tile([P, COLS], U8, tag="scales", align_bytes=64)
            for rows in (slice(0, 2 * P), slice(2 * P, 3 * P)):
                nc.vector.quantize_mx(
                    out=codes[:, rows].bitcast(FP8X4),
                    scales=scales[:, rows],
                    in_=grouped[:, rows, :].rearrange("p c t -> p (c t)"),
                )
            in_flight[("codes", unit)] = (codes, scales)

        def second_matmul(unit):
            e = unit % EXPERTS
            codes, scales = in_flight[("codes", unit)]
            o_ps = psum_o.tile([P, ROW_TILES, OUTPUTS], F32, tag="o")
            outs = slice(OUTPUTS * e, OUTPUTS * (e + 1))
            for r in range(ROW_TILES):
                rows = slice(P * r, P * (r + 1))
                nc.tensor.matmul_mx(
                    out=o_ps[:, r, :],
                    lhsT=codes[:, rows].bitcast(FP8X4),
                    lhsT_scale=scales[:, rows],
                    rhs=w2_codes[:, outs].bitcast(FP8X4),
                    rhs_scale=w2_scales[:, outs],
                    start=True,
                    stop=True,
                )
            in_flight[("o", unit)] = o_ps

        def leave_psum(unit):
            o_ps = in_flight[("o", unit)]
            res = results.tile([P, ROW_TILES, OUTPUTS], F32, tag="res")
            if unit % EXPERTS == 0:
                nc.scalar.activation(out=res[:], in_=o_ps[:], func=ACT.Sigmoid)
            else:
                nc.scalar.copy(out=res[:], in_=o_ps[:])
            in_flight[("res", unit)] = res

        def stretch(unit):
            res = in_flight[("res", unit)]
            (nc.vector if unit == UNITS - 2 else nc.gpsimd).tensor_scalar(out=res[:], in0=res[:], scalar1=1.2, scalar2=-0.1, op0=ALU.mult, op1=ALU.add)

        def clip_and_store(unit):
            j, e = divmod(unit, EXPERTS)
            res = in_flight[("res", unit)]
            if e == 0:
                (nc.vector if unit == UNITS - 2 else nc.gpsimd).tensor_scalar(
                    out=res[:], in0=res[:], scalar1=1.0, scalar2=0.0, op0=ALU.min, op1=ALU.max
                )
            out_gates = (out_0, out_1)[e].rearrange("b (half j) k -> b half j k", half=2)
            nc.sync.dma_start(out=out_gates[0:P, :, j, :], in_=res[:, 0:ROW_TILES:2, :])
            for half in range(2):
                nc.sync.dma_start(
                    out=out_gates[P:BATCH, half, j, :], in_=res[REST * half : REST * (half + 1), 1, :]
                )

        for u in range(WORDS):
            nc.tensor.transpose(out=bn_ps[:, u, :], in_=bn_words[:, u : HIDDEN // 2 : WORDS], identity=ident_words[:])
        nc.scalar.activation(
            out=rstd[:], in_=bn_parameter(0), func=ACT.Abs_reciprocal_sqrt, bias=eps[:, 0:1], scale=1.0
        )
        warm = const.tile([P, 1], F32)
        nc.scalar.activation(out=warm[:], in_=eps[:], func=ACT.Sigmoid)
        early, late, both = (0, 1), (2, 3), (0, 1, 2, 3)
        transpose_w1(0, early)
        transpose_le(0)
        transpose_w1(0, late)
        copy_w1(0, early)
        nc.vector.tensor_tensor(out=gain[:], in0=bn_parameter(1), in1=rstd[:], op=ALU.mult)
        transpose_w1(1, both)
        nc.vector.tensor_copy(out=leT[:, 0], in_=in_flight[("le", 0)][:])
        nc.vector.tensor_tensor(out=mean_gain[:], in0=bn_parameter(2), in1=gain[:], op=ALU.mult)
        copy_w1(0, late)
        first_matmul(0)
        transpose_le(1)
        nc.vector.tensor_tensor(out=shift[:], in0=bn_parameter(3), in1=mean_gain[:], op=ALU.subtract)
        copy_w1(1, both)

        def copy_le1():
            nc.vector.tensor_copy(out=leT[:, 1], in_=in_flight[("le", 1)][:])

        w2_grouped = const.tile([P, EXPERTS, OUTPUTS, PACK], BF16, align_bytes=64)
        w2_codes = const.tile([P, EXPERTS * OUTPUTS], U32, align_bytes=64)
        w2_scales = const.tile([P, EXPERTS * OUTPUTS], U8, align_bytes=64)
        w2_words = w2_rows[:].rearrange("k e h -> k (e h)").bitcast(F32).rearrange("k (e w) -> k e w", e=EXPERTS)

        def transpose_w2():
            w2_ps = psum_o.tile([P, EXPERTS, WORDS, OUTPUTS], F32, tag="o")
            for e in range(EXPERTS):
                for u in range(WORDS):
                    nc.tensor.transpose(
                        out=w2_ps[:, e, u, :], in_=w2_words[:, e, u : HIDDEN // 2 : WORDS], identity=ident_words[:]
                    )
            in_flight["w2"] = w2_ps

        def regroup_w2():
            nc.scalar.copy(
                out=w2_grouped[:]
                .rearrange("p e k t -> p (e k t)")
                .bitcast(F32)
                .rearrange("p (e k u) -> p e k u", e=EXPERTS, u=WORDS),
                in_=in_flight["w2"][:].rearrange("p e u k -> p e k u"),
            )

        def quantise_w2():
            nc.vector.quantize_mx(
                out=w2_codes[:].bitcast(FP8X4),
                scales=w2_scales[:],
                in_=w2_grouped[:].rearrange("p e k t -> p (e k t)"),
            )


        for step in range(UNITS + 3):
            turn_le = step % EXPERTS == 0 and 2 <= step and step + 2 < UNITS
            if turn_le:
                transpose_le((step + 2) // EXPERTS)
            if 0 <= step - 2 < UNITS:
                second_matmul(step - 2)
            if step + 1 < UNITS:
                first_matmul(step + 1)
            if step == 0:
                transpose_w2()
            if 0 <= step - 3:
                leave_psum(step - 3)
            if 0 <= step - 1 < UNITS - 1:
                regroup(step - 1)
            if step == UNITS:
                regroup_shared(step - 1)
            if step < UNITS:
                batchnorm(step)
            if step == 0:
                copy_le1()
            if step == 1:
                regroup_w2()
            if turn_le:
                copy_le((step + 2) // EXPERTS)
            if 0 <= step - 3 and (step - 3) % EXPERTS == 0:
                stretch(step - 3)
            if 0 <= step - 1 < UNITS:
                quantise(step - 1)
            if step == 1:
                quantise_w2()
            if 0 <= step - 3:
                clip_and_store(step - 3)
